import numpy as np
import ml_dtypes


def mxq(x, axis, fmt="e4m3"):
    dtype, down = {"e4m3": (ml_dtypes.float8_e4m3fn, 7), "e5m2": (ml_dtypes.float8_e5m2, 14)}[fmt]
    v = np.moveaxis(np.asarray(x, np.float32).astype(ml_dtypes.bfloat16).astype(np.float64), axis, -1)
    blocks = v.reshape(v.shape[:-1] + (-1, 32))
    amax = np.abs(blocks).max(-1, keepdims=True)
    byte = np.maximum(np.where(amax > 0, np.frexp(amax)[1] - 1 + 127, 0) - down, 1)
    scale = np.exp2(byte - 127.0)
    codes = (blocks / scale).astype(np.float32).astype(dtype).astype(np.float64)
    return np.moveaxis((codes * scale).reshape(v.shape), -1, axis)


WIDE = False


def mx_kscale(k):
    if not WIDE:
        return np.ones(k)
    levels = np.array([10, -10, 5, -5, 0])
    if k % 512:
        return np.exp2(np.random.permutation(np.resize(levels, k // 32))).repeat(32)
    a = np.empty((k // 512, 16))
    for p in range(k // 512):
        a[p, :8] = np.random.permutation(np.resize(levels, 8))
        for g in range(8):
            far = levels[np.abs(levels - a[p, g]) >= 10]
            a[p, g + 8] = far[np.random.randint(len(far))]
    return np.exp2(a.ravel()).repeat(32)


BF16 = ml_dtypes.bfloat16


def bf(x):
    return np.asarray(x, np.float32).astype(BF16)


def f64(x):
    return np.asarray(x).astype(np.float64)


N, C = 4096, 256
KV = 2 * C
SQRT2 = np.sqrt(2.0)
EPS = 1e-6


def setup_inputs():
    t = mx_kscale(KV)
    return {"s": bf(np.random.standard_normal((N, C))),
            "v": bf(np.random.standard_normal((N, C, 3))),
            "g_v": bf(np.random.standard_normal((N, KV)) * t),
            "wv": bf(np.random.standard_normal((KV, C)) / t[:, None]),
            "ln_g1": bf(1.0 + 0.1 * np.random.standard_normal(C))}


def reference(s, v, g_v, wv, ln_g1):
    s, v = f64(s), f64(v)
    sv = SQRT2 * s[..., None] * v
    vec = np.concatenate([v, sv], axis=1) * f64(g_v)[..., None]
    dv = (mxq(vec.transpose(0, 2, 1), 2, "e4m3") @ mxq(f64(wv), 0, "e4m3")) / np.sqrt(KV)
    y = v + dv.transpose(0, 2, 1)
    rms = np.sqrt(np.mean(y * y, axis=(1, 2), keepdims=True) + EPS)
    return y / rms * f64(ln_g1)[None, :, None]

@@ -1,0 +1,347 @@
+import math
+from contextlib import ExitStack
+
+import concourse.mybir as mybir
+from concourse.masks import make_identity
+
+BF16 = mybir.dt.bfloat16
+F32 = mybir.dt.float32
+U32 = mybir.dt.uint32
+U8 = mybir.dt.uint8
+FP8X4 = mybir.dt.float8_e4m3fn_x4
+MULT = mybir.AluOpType.mult
+ADD = mybir.AluOpType.add
+ACT = mybir.ActivationFunctionType
+
+P = 128
+HALF = P // 2
+POINTS = 4096
+C = 256
+DIMS = 3
+KV = 2 * C
+PACK = 4
+WORDS = C // PACK
+PARTS = 2
+TILES = POINTS // P
+GROUP = 2
+PAIRS = TILES // GROUP
+C_CHUNKS = C // P
+AHEAD = 2
+SG_AHEAD = AHEAD + 1
+LOAD_AHEAD = 6
+EPS = 1e-6
+
+FLOPS = 2 * POINTS * DIMS * KV * C
+
+
+def tile_selfinteraction_pb_t_kernel(tc, s, v, g_v, wv, ln_g1, out):
+    nc = tc.nc
+    with ExitStack() as ctx:
+        const = ctx.enter_context(tc.tile_pool(name="const", bufs=1))
+        sg_pool = ctx.enter_context(tc.tile_pool(name="sg_pool", bufs=3))
+        vt_pool = ctx.enter_context(tc.tile_pool(name="vt_pool", bufs=3))
+        mx_pool = ctx.enter_context(tc.tile_pool(name="mx_pool", bufs=2))
+        y_pool = ctx.enter_context(tc.tile_pool(name="y_pool", bufs=5))
+        o_pool = ctx.enter_context(tc.tile_pool(name="o_pool", bufs=8))
+        stat_pool = ctx.enter_context(tc.tile_pool(name="stat_pool", bufs=3))
+        flip_psum = ctx.enter_context(tc.psum_pool(name="flip_psum", bufs=2))
+        dv_psum = ctx.enter_context(tc.psum_pool(name="dv_psum", bufs=2))
+        ctx.enter_context(tc.manual_schedule())
+
+        s_dram = s.rearrange("(p i) c -> p i c", i=TILES)
+        g_dram = g_v.rearrange("(p i) m -> p i m", i=TILES)
+        v_dram = v.rearrange("(p i) c d -> p i (c d)", i=TILES)
+        out_dram = out.rearrange("(p i) c d -> p i c d", i=TILES)
+
+        s_sb = const.tile([P, TILES, C], BF16)
+        g0_sb = const.tile([P, TILES, C], BF16)
+        g1_sb = const.tile([P, TILES, C], BF16)
+        v_sb = const.tile([P, TILES, C * DIMS], BF16)
+        gain_sb = const.tile([P, C], BF16)
+        w_rows = const.tile([P, PACK, C], BF16)
+        w_rows_swapped = const.tile([P, PACK, C], BF16)
+
+        def load(j):
+            tiles = slice(j * GROUP, (j + 1) * GROUP)
+            nc.sync.dma_start(out=s_sb[:, tiles, :], in_=s_dram[:, tiles, :])
+            nc.sync.dma_start(out=g1_sb[:, tiles, :], in_=g_dram[:, tiles, C:KV])
+            nc.sync.dma_start(out=v_sb[:, tiles, :], in_=v_dram[:, tiles, :])
+            nc.sync.dma_start(out=g0_sb[:, tiles, :], in_=g_dram[:, tiles, 0:C])
+
+        load(0)
+        wv_view = wv.rearrange("(p t) c -> p t c", t=PACK)
+        nc.sync.dma_start(out=w_rows[:], in_=wv_view)
+        nc.sync.dma_start(out=w_rows_swapped[0:HALF], in_=wv_view[HALF:P])
+        nc.sync.dma_start(out=w_rows_swapped[HALF:P], in_=wv_view[0:HALF])
+        for j in range(1, LOAD_AHEAD):
+            load(j)
+            if j == 2:
+                nc.sync.dma_start(out=gain_sb[:], in_=ln_g1.partition_broadcast(P))
+
+        v_vals = v_sb[:].rearrange("p i (q f) -> p (i q) f", f=PACK * DIMS)
+        v_cd = v_sb[:].rearrange("p i (c d) -> p i c d", d=DIMS)
+        g0_words = g0_sb[:].bitcast(F32).rearrange("p i (q u) -> p (i q) u", u=PACK // 2)
+
+        ident_b = const.tile([P, P], BF16)
+        make_identity(nc, ident_b[:])
+        ident = const.tile([P, P], F32)
+        make_identity(nc, ident[:])
+        eps_sb = const.tile([P, 1], F32)
+        nc.vector.memset(eps_sb[:], EPS)
+        w_grouped = const.tile([P, PARTS * GROUP, C, PACK], BF16, align_bytes=64)
+        nc.vector.memset(w_grouped[:], 0.0)
+        table_warmer = const.tile([P, 1], F32)
+        nc.scalar.activation(out=table_warmer[:], in_=eps_sb[:], func=ACT.Abs_reciprocal_sqrt)
+
+        sg_of = {}
+        va_of = {}
+        vb_of = {}
+        sg_t_of = {}
+        v_t_of = {}
+        u_of = {}
+        u_codes_of = {}
+        u_scales_of = {}
+        dv_of = {}
+        y_of = {}
+        o_of = {}
+        sum_sq_of = {}
+        inv_rms_of = {}
+
+        def scalar_gates(j):
+            tiles = slice(j * GROUP, (j + 1) * GROUP)
+            sg = sg_pool.tile([P, GROUP * C], F32, tag="sg")
+            nc.gpsimd.tensor_tensor(
+                out=sg[:].rearrange("p (k c) -> p k c", k=GROUP),
+                in0=s_sb[:, tiles, :],
+                in1=g1_sb[:, tiles, :],
+                op=MULT,
+            )
+            sg_of[j] = sg
+
+        def flip_a(j):
+            va = flip_psum.tile([P, P * PACK], F32, tag="va")
+            bank = va[:].bitcast(BF16)
+            words = slice(j * P, (j + 1) * P)
+            for d in range(DIMS - 1):
+                for t in range(PACK):
+                    b = (d * PACK + t) * P
+                    nc.tensor.transpose(
+                        out=bank[:, b : b + P], in_=v_vals[:, words, DIMS * t + d], identity=ident_b[:]
+                    )
+            va_of[j] = va
+
+        def flip_b(j):
+            vb = flip_psum.tile([P, P * PACK], F32, tag="vb")
+            bank = vb[:].bitcast(BF16)
+            words = slice(j * P, (j + 1) * P)
+            for t in range(PACK):
+                nc.tensor.transpose(
+                    out=bank[:, t * P : (t + 1) * P],
+                    in_=v_vals[:, words, DIMS * t + DIMS - 1],
+                    identity=ident_b[:],
+                )
+            g0_t = vb[:, 2 * P : 4 * P].rearrange("p (n u) -> p n u", u=PACK // 2)
+            for u in range(PACK // 2):
+                nc.tensor.transpose(out=g0_t[:, :, u], in_=g0_words[:, words, u], identity=ident[:])
+            vb_of[j] = vb
+
+        def flip_c(j):
+            sg_t = flip_psum.tile([P, P, PACK], F32, tag="sg_t")
+            sg_words = sg_of[j][:].rearrange("p (w t) -> p w t", t=PACK)
+            for t in range(PACK):
+                nc.tensor.transpose(out=sg_t[:, :, t], in_=sg_words[:, :, t], identity=ident[:])
+            sg_t_of[j] = sg_t
+
+        def fetch_a(j):
+            v_t = vt_pool.tile([P, DIMS, P, PACK], BF16, tag="v_t")
+            nc.scalar.copy(
+                out=v_t[:, 0 : DIMS - 1, :, :],
+                in_=va_of[j][:].bitcast(BF16).rearrange("p (d t n) -> p d n t", t=PACK, n=P),
+            )
+            v_t_of[j] = v_t
+
+        def fetch_b(j):
+            nc.scalar.copy(
+                out=v_t_of[j][:, DIMS - 1, :, :],
+                in_=vb_of[j][:].bitcast(BF16)[:, 0 : PACK * P].rearrange("p (t n) -> p n t", t=PACK),
+            )
+
+        def product_0(j):
+            u = mx_pool.tile([P, PARTS, DIMS, P * PACK], BF16, align_bytes=64, tag="u")
+            nc.vector.tensor_tensor(
+                out=u[:, 0, :, :],
+                in0=vb_of[j][:]
+                .bitcast(BF16)[:, PACK * P : 2 * PACK * P]
+                .unsqueeze(1)
+                .to_broadcast([P, DIMS, PACK * P]),
+                in1=v_t_of[j][:].rearrange("p d n t -> p d (n t)"),
+                op=MULT,
+            )
+            u_of[j] = u
+
+        def product_1(j):
+            nc.vector.scalar_tensor_tensor(
+                out=u_of[j][:, 1, :, :],
+                in0=sg_t_of[j][:]
+                .rearrange("p n t -> p (n t)")
+                .unsqueeze(1)
+                .to_broadcast([P, DIMS, P * PACK]),
+                scalar=math.sqrt(2.0),
+                in1=v_t_of[j][:].rearrange("p d n t -> p d (n t)"),
+                op0=MULT,
+                op1=MULT,
+            )
+
+        def quantise(j):
+            columns = PARTS * DIMS * P
+            codes = mx_pool.tile([P, columns], U32, align_bytes=64, tag="codes")
+            scales = mx_pool.tile([P, columns], U8, align_bytes=64, tag="scales")
+            u = u_of[j][:].rearrange("p h d w -> p (h d w)")
+            for first, last in ((0, 4 * P), (4 * P, columns)):
+                nc.vector.quantize_mx(
+                    out=codes[:, first:last].bitcast(FP8X4),
+                    scales=scales[:, first:last],
+                    in_=u[:, first * PACK : last * PACK],
+                )
+            u_codes_of[j] = codes
+            u_scales_of[j] = scales
+
+        def project(j, k, chunk):
+            dv = dv_psum.tile([P, DIMS, P], F32, tag="dv")
+            for d in range(DIMS):
+                for h in range(PARTS):
+                    cols = slice((h * DIMS + d) * P, (h * DIMS + d + 1) * P)
+                    w_cols = slice((h * GROUP + k) * C + chunk * P, (h * GROUP + k) * C + (chunk + 1) * P)
+                    nc.tensor.matmul_mx(
+                        out=dv[:, d, :],
+                        lhsT=u_codes_of[j][:, cols].bitcast(FP8X4),
+                        lhsT_scale=u_scales_of[j][:, cols],
+                        rhs=wv_codes[:, w_cols].bitcast(FP8X4),
+                        rhs_scale=wv_scales[:, w_cols],
+                        start=(h == 0),
+                        stop=(h == PARTS - 1),
+                    )
+            dv_of[(j, k, chunk)] = dv
+
+        def residual(j, k, chunk):
+            if chunk == 0:
+                y = y_pool.tile([P, C, DIMS], F32, tag="y")
+                y_of[(j, k)] = y
+            cols = slice(chunk * P, (chunk + 1) * P)
+            nc.vector.scalar_tensor_tensor(
+                out=y_of[(j, k)][:, cols, :],
+                in0=dv_of[(j, k, chunk)][:].rearrange("p d c -> p c d"),
+                scalar=1.0 / math.sqrt(KV),
+                in1=v_cd[:, j * GROUP + k, cols, :],
+                op0=MULT,
+                op1=ADD,
+            )
+
+        def sum_squares(j, k):
+            if k == 0:
+                sum_sq = stat_pool.tile([P, GROUP], F32, tag="sum_sq")
+                sum_sq_of[j] = sum_sq
+            squares = stat_pool.tile([P, C, DIMS], BF16, tag="squares")
+            nc.scalar.activation(
+                out=squares[:], in_=y_of[(j, k)][:], func=ACT.Square, accum_out=sum_sq_of[j][:, k : k + 1]
+            )
+
+        def inverse_rms(j):
+            inv_rms = stat_pool.tile([P, GROUP], F32, tag="inv_rms")
+            nc.scalar.activation(
+                out=inv_rms[:],
+                in_=sum_sq_of[j][:],
+                func=ACT.Abs_reciprocal_sqrt,
+                bias=eps_sb[:],
+                scale=1.0 / (C * DIMS),
+            )
+            inv_rms_of[j] = inv_rms
+
+        def apply_gain(j, k):
+            o = o_pool.tile([P, C, DIMS], F32, tag="o")
+            nc.gpsimd.tensor_tensor(
+                out=o[:],
+                in0=y_of[(j, k)][:],
+                in1=gain_sb[:].unsqueeze(2).to_broadcast([P, C, DIMS]),
+                op=MULT,
+            )
+            o_of[(j, k)] = o
+
+        def normalise_and_store(j, k):
+            o = o_of[(j, k)]
+            nc.scalar.activation(out=o[:], in_=o[:], func=ACT.Copy, scale=inv_rms_of[j][:, k : k + 1])
+            nc.sync.dma_start(out=out_dram[:, j * GROUP + k, :, :], in_=o[:])
+
+        for j in range(SG_AHEAD):
+            scalar_gates(j)
+        for j in range(AHEAD):
+            flip_a(j)
+            flip_b(j)
+            flip_c(j)
+            fetch_a(j)
+            if j == 0:
+                fetch_b(j)
+
+        for h in range(PARTS):
+            for k in range(GROUP):
+                rows = slice(k * HALF, (k + 1) * HALF)
+                source = w_rows if h == k else w_rows_swapped
+                nc.vector.tensor_copy(
+                    out=w_grouped[rows, h * GROUP + k, :, :],
+                    in_=source[rows, :, :].rearrange("q t c -> q c t"),
+                )
+        wv_codes = const.tile([P, PARTS * GROUP * C], U32, align_bytes=64)
+        wv_scales = const.tile([P, PARTS * GROUP * C], U8, align_bytes=64)
+        nc.vector.quantize_mx(
+            out=wv_codes[:].bitcast(FP8X4),
+            scales=wv_scales[:],
+            in_=w_grouped[:].rearrange("q o c t -> q (o c t)"),
+        )
+
+        for j in range(PAIRS + 2):
+            now = j < PAIRS
+            y_now = 0 <= j - 1 < PAIRS
+            o_now = 0 <= j - 2 < PAIRS
+            flip_now = j + AHEAD < PAIRS
+            if j + LOAD_AHEAD < PAIRS:
+                load(j + LOAD_AHEAD)
+            if y_now:
+                project(j - 1, 0, 0)
+                project(j - 1, 0, 1)
+            if now:
+                product_0(j)
+            if y_now:
+                residual(j - 1, 0, 0)
+                residual(j - 1, 0, 1)
+            if flip_now:
+                flip_a(j + AHEAD)
+            if y_now:
+                project(j - 1, 1, 0)
+                project(j - 1, 1, 1)
+            if now:
+                product_1(j)
+            if flip_now:
+                flip_b(j + AHEAD)
+                flip_c(j + AHEAD)
+            if o_now:
+                apply_gain(j - 2, 1)
+                sum_squares(j - 2, 1)
+                inverse_rms(j - 2)
+            if j + SG_AHEAD < PAIRS:
+                scalar_gates(j + SG_AHEAD)
+            if j + 1 < PAIRS:
+                fetch_b(j + 1)
+            if o_now:
+                normalise_and_store(j - 2, 0)
+            if y_now:
+                apply_gain(j - 1, 0)
+                sum_squares(j - 1, 0)
+            if flip_now:
+                fetch_a(j + AHEAD)
+            if o_now:
+                normalise_and_store(j - 2, 1)
+            if y_now:
+                residual(j - 1, 1, 0)
+                residual(j - 1, 1, 1)
+            if now:
+                quantise(j)

@@ -25,6 +25,8 @@ PARTS = 2
 TILES = POINTS // P
 GROUP = 2
 PAIRS = TILES // GROUP
+COLUMNS = PARTS * DIMS * P
+EARLY = 2 * P
 C_CHUNKS = C // P
 AHEAD = 2
 SG_AHEAD = AHEAD + 1
@@ -107,16 +109,16 @@ def tile_selfinteraction_pb_t_kernel(tc, s, v, g_v, wv, ln_g1, out):
         sum_sq_of = {}
         inv_rms_of = {}
 
-        def scalar_gates(j):
-            tiles = slice(j * GROUP, (j + 1) * GROUP)
-            sg = sg_pool.tile([P, GROUP * C], F32, tag="sg")
+        def scalar_gates(j, k):
+            if k == 0:
+                sg = sg_pool.tile([P, GROUP * C], F32, tag="sg")
+                sg_of[j] = sg
             nc.gpsimd.tensor_tensor(
-                out=sg[:].rearrange("p (k c) -> p k c", k=GROUP),
-                in0=s_sb[:, tiles, :],
-                in1=g1_sb[:, tiles, :],
+                out=sg_of[j][:, k * C : (k + 1) * C],
+                in0=s_sb[:, j * GROUP + k, :],
+                in1=g1_sb[:, j * GROUP + k, :],
                 op=MULT,
             )
-            sg_of[j] = sg
 
         def flip_a(j):
             va = flip_psum.tile([P, P * PACK], F32, tag="va")
@@ -192,19 +194,17 @@ def tile_selfinteraction_pb_t_kernel(tc, s, v, g_v, wv, ln_g1, out):
                 op1=MULT,
             )
 
-        def quantise(j):
-            columns = PARTS * DIMS * P
-            codes = mx_pool.tile([P, columns], U32, align_bytes=64, tag="codes")
-            scales = mx_pool.tile([P, columns], U8, align_bytes=64, tag="scales")
-            u = u_of[j][:].rearrange("p h d w -> p (h d w)")
-            for first, last in ((0, 4 * P), (4 * P, columns)):
-                nc.vector.quantize_mx(
-                    out=codes[:, first:last].bitcast(FP8X4),
-                    scales=scales[:, first:last],
-                    in_=u[:, first * PACK : last * PACK],
-                )
-            u_codes_of[j] = codes
-            u_scales_of[j] = scales
+        def quantise(j, first, last):
+            if first == 0:
+                codes = mx_pool.tile([P, COLUMNS], U32, align_bytes=64, tag="codes")
+                scales = mx_pool.tile([P, COLUMNS], U8, align_bytes=64, tag="scales")
+                u_codes_of[j] = codes
+                u_scales_of[j] = scales
+            nc.vector.quantize_mx(
+                out=u_codes_of[j][:, first:last].bitcast(FP8X4),
+                scales=u_scales_of[j][:, first:last],
+                in_=u_of[j][:].rearrange("p h d w -> p (h d w)")[:, first * PACK : last * PACK],
+            )
 
         def project(j, k, chunk):
             dv = dv_psum.tile([P, DIMS, P], F32, tag="dv")
@@ -273,7 +273,8 @@ def tile_selfinteraction_pb_t_kernel(tc, s, v, g_v, wv, ln_g1, out):
             nc.sync.dma_start(out=out_dram[:, j * GROUP + k, :, :], in_=o[:])
 
         for j in range(SG_AHEAD):
-            scalar_gates(j)
+            for k in range(GROUP):
+                scalar_gates(j, k)
         for j in range(AHEAD):
             flip_a(j)
             flip_b(j)
@@ -305,6 +306,9 @@ def tile_selfinteraction_pb_t_kernel(tc, s, v, g_v, wv, ln_g1, out):
             flip_now = j + AHEAD < PAIRS
             if j + LOAD_AHEAD < PAIRS:
                 load(j + LOAD_AHEAD)
+            sg_now = j + SG_AHEAD < PAIRS
+            if o_now:
+                residual(j - 2, 1, 1)
             if y_now:
                 project(j - 1, 0, 0)
                 project(j - 1, 0, 1)
@@ -313,6 +317,8 @@ def tile_selfinteraction_pb_t_kernel(tc, s, v, g_v, wv, ln_g1, out):
             if y_now:
                 residual(j - 1, 0, 0)
                 residual(j - 1, 0, 1)
+            if now:
+                quantise(j, 0, EARLY)
             if flip_now:
                 flip_a(j + AHEAD)
             if y_now:
@@ -323,12 +329,16 @@ def tile_selfinteraction_pb_t_kernel(tc, s, v, g_v, wv, ln_g1, out):
             if flip_now:
                 flip_b(j + AHEAD)
                 flip_c(j + AHEAD)
+            if y_now:
+                residual(j - 1, 1, 0)
+            if now:
+                quantise(j, EARLY, COLUMNS)
+            if sg_now:
+                scalar_gates(j + SG_AHEAD, 0)
             if o_now:
                 apply_gain(j - 2, 1)
                 sum_squares(j - 2, 1)
                 inverse_rms(j - 2)
-            if j + SG_AHEAD < PAIRS:
-                scalar_gates(j + SG_AHEAD)
             if j + 1 < PAIRS:
                 fetch_b(j + 1)
             if o_now:
@@ -340,8 +350,5 @@ def tile_selfinteraction_pb_t_kernel(tc, s, v, g_v, wv, ln_g1, out):
                 fetch_a(j + AHEAD)
             if o_now:
                 normalise_and_store(j - 2, 1)
-            if y_now:
-                residual(j - 1, 1, 0)
-                residual(j - 1, 1, 1)
-            if now:
-                quantise(j)
+            if sg_now:
+                scalar_gates(j + SG_AHEAD, 1)

@@ -111,12 +111,12 @@ def tile_selfinteraction_pb_t_kernel(tc, s, v, g_v, wv, ln_g1, out):
 
         def scalar_gates(j, k):
             if k == 0:
-                sg = sg_pool.tile([P, GROUP * C], F32, tag="sg")
+                sg = sg_pool.tile([P, PACK, P], F32, tag="sg")
                 sg_of[j] = sg
             nc.gpsimd.tensor_tensor(
-                out=sg_of[j][:, k * C : (k + 1) * C],
-                in0=s_sb[:, j * GROUP + k, :],
-                in1=g1_sb[:, j * GROUP + k, :],
+                out=sg_of[j][:, :, k * WORDS : (k + 1) * WORDS],
+                in0=s_sb[:, j * GROUP + k, :].rearrange("p (q t) -> p t q", t=PACK),
+                in1=g1_sb[:, j * GROUP + k, :].rearrange("p (q t) -> p t q", t=PACK),
                 op=MULT,
             )
 
@@ -142,16 +142,15 @@ def tile_selfinteraction_pb_t_kernel(tc, s, v, g_v, wv, ln_g1, out):
                     in_=v_vals[:, words, DIMS * t + DIMS - 1],
                     identity=ident_b[:],
                 )
-            g0_t = vb[:, 2 * P : 4 * P].rearrange("p (n u) -> p n u", u=PACK // 2)
             for u in range(PACK // 2):
-                nc.tensor.transpose(out=g0_t[:, :, u], in_=g0_words[:, words, u], identity=ident[:])
+                b = (2 + u) * P
+                nc.tensor.transpose(out=vb[:, b : b + P], in_=g0_words[:, words, u], identity=ident[:])
             vb_of[j] = vb
 
         def flip_c(j):
-            sg_t = flip_psum.tile([P, P, PACK], F32, tag="sg_t")
-            sg_words = sg_of[j][:].rearrange("p (w t) -> p w t", t=PACK)
+            sg_t = flip_psum.tile([P, PACK, P], F32, tag="sg_t")
             for t in range(PACK):
-                nc.tensor.transpose(out=sg_t[:, :, t], in_=sg_words[:, :, t], identity=ident[:])
+                nc.tensor.transpose(out=sg_t[:, t, :], in_=sg_of[j][:, t, :], identity=ident[:])
             sg_t_of[j] = sg_t
 
         def fetch_a(j):
@@ -170,29 +169,26 @@ def tile_selfinteraction_pb_t_kernel(tc, s, v, g_v, wv, ln_g1, out):
 
         def product_0(j):
             u = mx_pool.tile([P, PARTS, DIMS, P * PACK], BF16, align_bytes=64, tag="u")
-            nc.vector.tensor_tensor(
-                out=u[:, 0, :, :],
-                in0=vb_of[j][:]
-                .bitcast(BF16)[:, PACK * P : 2 * PACK * P]
-                .unsqueeze(1)
-                .to_broadcast([P, DIMS, PACK * P]),
-                in1=v_t_of[j][:].rearrange("p d n t -> p d (n t)"),
-                op=MULT,
-            )
+            gates = vb_of[j][:].bitcast(BF16)[:, PACK * P : 2 * PACK * P]
+            for d in range(DIMS):
+                nc.vector.tensor_tensor(
+                    out=u[:, 0, d, :].rearrange("p (n u e) -> p n u e", u=2, e=2),
+                    in0=gates.rearrange("p (u n e) -> p n u e", u=2, e=2),
+                    in1=v_t_of[j][:, d, :, :].rearrange("p n (u e) -> p n u e", e=2),
+                    op=MULT,
+                )
             u_of[j] = u
 
         def product_1(j):
-            nc.vector.scalar_tensor_tensor(
-                out=u_of[j][:, 1, :, :],
-                in0=sg_t_of[j][:]
-                .rearrange("p n t -> p (n t)")
-                .unsqueeze(1)
-                .to_broadcast([P, DIMS, P * PACK]),
-                scalar=math.sqrt(2.0),
-                in1=v_t_of[j][:].rearrange("p d n t -> p d (n t)"),
-                op0=MULT,
-                op1=MULT,
-            )
+            for d in range(DIMS):
+                nc.vector.scalar_tensor_tensor(
+                    out=u_of[j][:, 1, d, :].rearrange("p (n t) -> p n t", t=PACK),
+                    in0=sg_t_of[j][:].rearrange("p t n -> p n t"),
+                    scalar=math.sqrt(2.0),
+                    in1=v_t_of[j][:, d, :, :],
+                    op0=MULT,
+                    op1=MULT,
+                )
 
         def quantise(j, first, last):
             if first == 0:

@@ -27,7 +27,6 @@ GROUP = 2
 PAIRS = TILES // GROUP
 COLUMNS = PARTS * DIMS * P
 EARLY = 2 * P
-C_CHUNKS = C // P
 AHEAD = 2
 SG_AHEAD = AHEAD + 1
 LOAD_AHEAD = 6
@@ -43,11 +42,12 @@ def tile_selfinteraction_pb_t_kernel(tc, s, v, g_v, wv, ln_g1, out):
         sg_pool = ctx.enter_context(tc.tile_pool(name="sg_pool", bufs=3))
         vt_pool = ctx.enter_context(tc.tile_pool(name="vt_pool", bufs=3))
         mx_pool = ctx.enter_context(tc.tile_pool(name="mx_pool", bufs=2))
-        y_pool = ctx.enter_context(tc.tile_pool(name="y_pool", bufs=5))
-        o_pool = ctx.enter_context(tc.tile_pool(name="o_pool", bufs=8))
+        y_pool = ctx.enter_context(tc.tile_pool(name="y_pool", bufs=4))
+        o_pool = ctx.enter_context(tc.tile_pool(name="o_pool", bufs=10))
         stat_pool = ctx.enter_context(tc.tile_pool(name="stat_pool", bufs=3))
+        va_psum = ctx.enter_context(tc.psum_pool(name="va_psum", bufs=1))
         flip_psum = ctx.enter_context(tc.psum_pool(name="flip_psum", bufs=2))
-        dv_psum = ctx.enter_context(tc.psum_pool(name="dv_psum", bufs=2))
+        dv_psum = ctx.enter_context(tc.psum_pool(name="dv_psum", bufs=DIMS))
         ctx.enter_context(tc.manual_schedule())
 
         s_dram = s.rearrange("(p i) c -> p i c", i=TILES)
@@ -121,7 +121,7 @@ def tile_selfinteraction_pb_t_kernel(tc, s, v, g_v, wv, ln_g1, out):
             )
 
         def flip_a(j):
-            va = flip_psum.tile([P, P * PACK], F32, tag="va")
+            va = va_psum.tile([P, P * PACK], F32, tag="va")
             bank = va[:].bitcast(BF16)
             words = slice(j * P, (j + 1) * P)
             for d in range(DIMS - 1):
@@ -202,33 +202,31 @@ def tile_selfinteraction_pb_t_kernel(tc, s, v, g_v, wv, ln_g1, out):
                 in_=u_of[j][:].rearrange("p h d w -> p (h d w)")[:, first * PACK : last * PACK],
             )
 
-        def project(j, k, chunk):
-            dv = dv_psum.tile([P, DIMS, P], F32, tag="dv")
-            for d in range(DIMS):
-                for h in range(PARTS):
-                    cols = slice((h * DIMS + d) * P, (h * DIMS + d + 1) * P)
-                    w_cols = slice((h * GROUP + k) * C + chunk * P, (h * GROUP + k) * C + (chunk + 1) * P)
-                    nc.tensor.matmul_mx(
-                        out=dv[:, d, :],
-                        lhsT=u_codes_of[j][:, cols].bitcast(FP8X4),
-                        lhsT_scale=u_scales_of[j][:, cols],
-                        rhs=wv_codes[:, w_cols].bitcast(FP8X4),
-                        rhs_scale=wv_scales[:, w_cols],
-                        start=(h == 0),
-                        stop=(h == PARTS - 1),
-                    )
-            dv_of[(j, k, chunk)] = dv
+        def project(j, d):
+            dv = dv_psum.tile([P, GROUP, C], F32, tag="dv")
+            for h in range(PARTS):
+                cols = slice((h * DIMS + d) * P, (h * DIMS + d + 1) * P)
+                w_cols = slice(h * GROUP * C, (h + 1) * GROUP * C)
+                nc.tensor.matmul_mx(
+                    out=dv[:].rearrange("p k c -> p (k c)"),
+                    lhsT=u_codes_of[j][:, cols].bitcast(FP8X4),
+                    lhsT_scale=u_scales_of[j][:, cols],
+                    rhs=wv_codes[:, w_cols].bitcast(FP8X4),
+                    rhs_scale=wv_scales[:, w_cols],
+                    start=(h == 0),
+                    stop=(h == PARTS - 1),
+                )
+            dv_of[(j, d)] = dv
 
-        def residual(j, k, chunk):
-            if chunk == 0:
-                y = y_pool.tile([P, C, DIMS], F32, tag="y")
-                y_of[(j, k)] = y
-            cols = slice(chunk * P, (chunk + 1) * P)
+        def residual(j, d):
+            if d == 0:
+                y = y_pool.tile([P, GROUP, DIMS, C], F32, tag="y")
+                y_of[j] = y
             nc.vector.scalar_tensor_tensor(
-                out=y_of[(j, k)][:, cols, :],
-                in0=dv_of[(j, k, chunk)][:].rearrange("p d c -> p c d"),
+                out=y_of[j][:, :, d, :],
+                in0=dv_of[(j, d)][:],
                 scalar=1.0 / math.sqrt(KV),
-                in1=v_cd[:, j * GROUP + k, cols, :],
+                in1=v_cd[:, j * GROUP : (j + 1) * GROUP, :, d],
                 op0=MULT,
                 op1=ADD,
             )
@@ -237,9 +235,9 @@ def tile_selfinteraction_pb_t_kernel(tc, s, v, g_v, wv, ln_g1, out):
             if k == 0:
                 sum_sq = stat_pool.tile([P, GROUP], F32, tag="sum_sq")
                 sum_sq_of[j] = sum_sq
-            squares = stat_pool.tile([P, C, DIMS], BF16, tag="squares")
+            squares = stat_pool.tile([P, DIMS, C], BF16, tag="squares")
             nc.scalar.activation(
-                out=squares[:], in_=y_of[(j, k)][:], func=ACT.Square, accum_out=sum_sq_of[j][:, k : k + 1]
+                out=squares[:], in_=y_of[j][:, k, :, :], func=ACT.Square, accum_out=sum_sq_of[j][:, k : k + 1]
             )
 
         def inverse_rms(j):
@@ -257,7 +255,7 @@ def tile_selfinteraction_pb_t_kernel(tc, s, v, g_v, wv, ln_g1, out):
             o = o_pool.tile([P, C, DIMS], F32, tag="o")
             nc.gpsimd.tensor_tensor(
                 out=o[:],
-                in0=y_of[(j, k)][:],
+                in0=y_of[j][:, k, :, :].rearrange("p d c -> p c d"),
                 in1=gain_sb[:].unsqueeze(2).to_broadcast([P, C, DIMS]),
                 op=MULT,
             )
@@ -276,8 +274,7 @@ def tile_selfinteraction_pb_t_kernel(tc, s, v, g_v, wv, ln_g1, out):
             flip_b(j)
             flip_c(j)
             fetch_a(j)
-            if j == 0:
-                fetch_b(j)
+            fetch_b(j)
 
         for h in range(PARTS):
             for k in range(GROUP):
@@ -295,56 +292,58 @@ def tile_selfinteraction_pb_t_kernel(tc, s, v, g_v, wv, ln_g1, out):
             in_=w_grouped[:].rearrange("q o c t -> q (o c t)"),
         )
 
-        for j in range(PAIRS + 2):
+        for j in range(PAIRS + 3):
             now = j < PAIRS
             y_now = 0 <= j - 1 < PAIRS
-            o_now = 0 <= j - 2 < PAIRS
+            z_now = 0 <= j - 2 < PAIRS
+            o_now = 0 <= j - 3 < PAIRS
             flip_now = j + AHEAD < PAIRS
+            sg_now = j + SG_AHEAD < PAIRS
             if j + LOAD_AHEAD < PAIRS:
                 load(j + LOAD_AHEAD)
-            sg_now = j + SG_AHEAD < PAIRS
-            if o_now:
-                residual(j - 2, 1, 1)
+            if z_now:
+                residual(j - 2, 2)
             if y_now:
-                project(j - 1, 0, 0)
-                project(j - 1, 0, 1)
+                project(j - 1, 0)
             if now:
                 product_0(j)
-            if y_now:
-                residual(j - 1, 0, 0)
-                residual(j - 1, 0, 1)
-            if now:
-                quantise(j, 0, EARLY)
             if flip_now:
                 flip_a(j + AHEAD)
             if y_now:
-                project(j - 1, 1, 0)
-                project(j - 1, 1, 1)
+                residual(j - 1, 0)
+                project(j - 1, 1)
+            if now:
+                quantise(j, 0, EARLY)
+            if flip_now:
+                flip_b(j + AHEAD)
+            if y_now:
+                project(j - 1, 2)
             if now:
                 product_1(j)
             if flip_now:
-                flip_b(j + AHEAD)
                 flip_c(j + AHEAD)
             if y_now:
-                residual(j - 1, 1, 0)
+                residual(j - 1, 1)
             if now:
                 quantise(j, EARLY, COLUMNS)
+            if z_now:
+                apply_gain(j - 2, 0)
             if sg_now:
                 scalar_gates(j + SG_AHEAD, 0)
-            if o_now:
+            if z_now:
                 apply_gain(j - 2, 1)
-                sum_squares(j - 2, 1)
-                inverse_rms(j - 2)
-            if j + 1 < PAIRS:
-                fetch_b(j + 1)
-            if o_now:
-                normalise_and_store(j - 2, 0)
-            if y_now:
-                apply_gain(j - 1, 0)
-                sum_squares(j - 1, 0)
-            if flip_now:
-                fetch_a(j + AHEAD)
-            if o_now:
-                normalise_and_store(j - 2, 1)
             if sg_now:
                 scalar_gates(j + SG_AHEAD, 1)
+            if o_now:
+                normalise_and_store(j - 3, 0)
+            if z_now:
+                sum_squares(j - 2, 0)
+            if flip_now:
+                fetch_a(j + AHEAD)
+            if z_now:
+                sum_squares(j - 2, 1)
+                inverse_rms(j - 2)
+            if o_now:
+                normalise_and_store(j - 3, 1)
+            if flip_now:
+                fetch_b(j + AHEAD)

@@ -28,8 +28,10 @@ PAIRS = TILES // GROUP
 COLUMNS = PARTS * DIMS * P
 EARLY = 2 * P
 AHEAD = 2
-SG_AHEAD = AHEAD + 1
+SG_LEAD = 19
+SG_PAIRS = 10
 LOAD_AHEAD = 6
+GATES_AHEAD = 10
 EPS = 1e-6
 
 FLOPS = 2 * POINTS * DIMS * KV * C
@@ -39,11 +41,12 @@ def tile_selfinteraction_pb_t_kernel(tc, s, v, g_v, wv, ln_g1, out):
     nc = tc.nc
     with ExitStack() as ctx:
         const = ctx.enter_context(tc.tile_pool(name="const", bufs=1))
-        sg_pool = ctx.enter_context(tc.tile_pool(name="sg_pool", bufs=3))
+        sg_pool = ctx.enter_context(tc.tile_pool(name="sg_pool", bufs=SG_PAIRS))
         vt_pool = ctx.enter_context(tc.tile_pool(name="vt_pool", bufs=3))
         mx_pool = ctx.enter_context(tc.tile_pool(name="mx_pool", bufs=2))
         y_pool = ctx.enter_context(tc.tile_pool(name="y_pool", bufs=4))
-        o_pool = ctx.enter_context(tc.tile_pool(name="o_pool", bufs=10))
+        o_pool = ctx.enter_context(tc.tile_pool(name="o_pool", bufs=5))
+        z_pool = ctx.enter_context(tc.tile_pool(name="z_pool", bufs=5))
         stat_pool = ctx.enter_context(tc.tile_pool(name="stat_pool", bufs=3))
         va_psum = ctx.enter_context(tc.psum_pool(name="va_psum", bufs=1))
         flip_psum = ctx.enter_context(tc.psum_pool(name="flip_psum", bufs=2))
@@ -63,21 +66,28 @@ def tile_selfinteraction_pb_t_kernel(tc, s, v, g_v, wv, ln_g1, out):
         w_rows = const.tile([P, PACK, C], BF16)
         w_rows_swapped = const.tile([P, PACK, C], BF16)
 
-        def load(j):
-            tiles = slice(j * GROUP, (j + 1) * GROUP)
+        def load_gates(first, last):
+            tiles = slice(first * GROUP, last * GROUP)
             nc.sync.dma_start(out=s_sb[:, tiles, :], in_=s_dram[:, tiles, :])
             nc.sync.dma_start(out=g1_sb[:, tiles, :], in_=g_dram[:, tiles, C:KV])
+
+        def load_vectors(j):
+            tiles = slice(j * GROUP, (j + 1) * GROUP)
             nc.sync.dma_start(out=v_sb[:, tiles, :], in_=v_dram[:, tiles, :])
             nc.sync.dma_start(out=g0_sb[:, tiles, :], in_=g_dram[:, tiles, 0:C])
 
-        load(0)
+        load_gates(0, 1)
+        load_vectors(0)
         wv_view = wv.rearrange("(p t) c -> p t c", t=PACK)
         nc.sync.dma_start(out=w_rows[:], in_=wv_view)
         nc.sync.dma_start(out=w_rows_swapped[0:HALF], in_=wv_view[HALF:P])
         nc.sync.dma_start(out=w_rows_swapped[HALF:P], in_=wv_view[0:HALF])
-        for j in range(1, LOAD_AHEAD):
-            load(j)
-            if j == 2:
+        load_gates(1, 2)
+        load_vectors(1)
+        for j in range(2, LOAD_AHEAD):
+            load_gates(2 * j - 2, 2 * j)
+            load_vectors(j)
+            if j == 3:
                 nc.sync.dma_start(out=gain_sb[:], in_=ln_g1.partition_broadcast(P))
 
         v_vals = v_sb[:].rearrange("p i (q f) -> p (i q) f", f=PACK * DIMS)
@@ -109,14 +119,15 @@ def tile_selfinteraction_pb_t_kernel(tc, s, v, g_v, wv, ln_g1, out):
         sum_sq_of = {}
         inv_rms_of = {}
 
-        def scalar_gates(j, k):
+        def scalar_gates(i):
+            j, k = divmod(i, GROUP)
             if k == 0:
                 sg = sg_pool.tile([P, PACK, P], F32, tag="sg")
                 sg_of[j] = sg
             nc.gpsimd.tensor_tensor(
                 out=sg_of[j][:, :, k * WORDS : (k + 1) * WORDS],
-                in0=s_sb[:, j * GROUP + k, :].rearrange("p (q t) -> p t q", t=PACK),
-                in1=g1_sb[:, j * GROUP + k, :].rearrange("p (q t) -> p t q", t=PACK),
+                in0=s_sb[:, i, :].rearrange("p (q t) -> p t q", t=PACK),
+                in1=g1_sb[:, i, :].rearrange("p (q t) -> p t q", t=PACK),
                 op=MULT,
             )
 
@@ -218,15 +229,15 @@ def tile_selfinteraction_pb_t_kernel(tc, s, v, g_v, wv, ln_g1, out):
                 )
             dv_of[(j, d)] = dv
 
-        def residual(j, d):
-            if d == 0:
+        def residual(j, k, d):
+            if k == 0 and d == 0:
                 y = y_pool.tile([P, GROUP, DIMS, C], F32, tag="y")
                 y_of[j] = y
             nc.vector.scalar_tensor_tensor(
-                out=y_of[j][:, :, d, :],
-                in0=dv_of[(j, d)][:],
+                out=y_of[j][:, k, d, :],
+                in0=dv_of[(j, d)][:, k, :],
                 scalar=1.0 / math.sqrt(KV),
-                in1=v_cd[:, j * GROUP : (j + 1) * GROUP, :, d],
+                in1=v_cd[:, j * GROUP + k, :, d],
                 op0=MULT,
                 op1=ADD,
             )
@@ -252,23 +263,42 @@ def tile_selfinteraction_pb_t_kernel(tc, s, v, g_v, wv, ln_g1, out):
             inv_rms_of[j] = inv_rms
 
         def apply_gain(j, k):
-            o = o_pool.tile([P, C, DIMS], F32, tag="o")
+            o = o_pool.tile([P, DIMS, C], F32, tag="o")
             nc.gpsimd.tensor_tensor(
                 out=o[:],
-                in0=y_of[j][:, k, :, :].rearrange("p d c -> p c d"),
-                in1=gain_sb[:].unsqueeze(2).to_broadcast([P, C, DIMS]),
+                in0=y_of[j][:, k, :, :],
+                in1=gain_sb[:].unsqueeze(1).to_broadcast([P, DIMS, C]),
                 op=MULT,
             )
             o_of[(j, k)] = o
 
-        def normalise_and_store(j, k):
-            o = o_of[(j, k)]
-            nc.scalar.activation(out=o[:], in_=o[:], func=ACT.Copy, scale=inv_rms_of[j][:, k : k + 1])
-            nc.sync.dma_start(out=out_dram[:, j * GROUP + k, :, :], in_=o[:])
+        def store(j, k, z):
+            nc.sync.dma_start(out=out_dram[:, j * GROUP + k, :, :], in_=z[:])
 
-        for j in range(SG_AHEAD):
-            for k in range(GROUP):
-                scalar_gates(j, k)
+        def normalise(j, k):
+            z = z_pool.tile([P, C, DIMS], F32, tag="z")
+            nc.scalar.activation(
+                out=z[:],
+                in_=o_of[(j, k)][:].rearrange("p d c -> p c d"),
+                func=ACT.Copy,
+                scale=inv_rms_of[j][:, k : k + 1],
+            )
+            store(j, k, z)
+
+        def normalise_with_gain(j, k):
+            z = z_pool.tile([P, C, DIMS], F32, tag="z")
+            nc.vector.scalar_tensor_tensor(
+                out=z[:],
+                in0=y_of[j][:, k, :, :].rearrange("p d c -> p c d"),
+                scalar=inv_rms_of[j][:, k : k + 1],
+                in1=gain_sb[:].unsqueeze(2).to_broadcast([P, C, DIMS]),
+                op0=MULT,
+                op1=MULT,
+            )
+            store(j, k, z)
+
+        for i in range(SG_LEAD):
+            scalar_gates(i)
         for j in range(AHEAD):
             flip_a(j)
             flip_b(j)
@@ -298,52 +328,51 @@ def tile_selfinteraction_pb_t_kernel(tc, s, v, g_v, wv, ln_g1, out):
             z_now = 0 <= j - 2 < PAIRS
             o_now = 0 <= j - 3 < PAIRS
             flip_now = j + AHEAD < PAIRS
-            sg_now = j + SG_AHEAD < PAIRS
             if j + LOAD_AHEAD < PAIRS:
-                load(j + LOAD_AHEAD)
-            if z_now:
-                residual(j - 2, 2)
-            if y_now:
-                project(j - 1, 0)
-            if now:
-                product_0(j)
+                load_vectors(j + LOAD_AHEAD)
+            if j + GATES_AHEAD < PAIRS:
+                load_gates(j + GATES_AHEAD, j + GATES_AHEAD + 1)
             if flip_now:
                 flip_a(j + AHEAD)
+            if now:
+                product_0(j)
+            if z_now:
+                for d in range(DIMS):
+                    residual(j - 2, 1, d)
             if y_now:
-                residual(j - 1, 0)
-                project(j - 1, 1)
+                for d in range(DIMS):
+                    project(j - 1, d)
             if now:
                 quantise(j, 0, EARLY)
-            if flip_now:
-                flip_b(j + AHEAD)
-            if y_now:
-                project(j - 1, 2)
-            if now:
                 product_1(j)
             if flip_now:
+                flip_b(j + AHEAD)
                 flip_c(j + AHEAD)
             if y_now:
-                residual(j - 1, 1)
+                for d in range(DIMS):
+                    residual(j - 1, 0, d)
             if now:
                 quantise(j, EARLY, COLUMNS)
+            last = j - 2 == PAIRS - 1
             if z_now:
                 apply_gain(j - 2, 0)
-            if sg_now:
-                scalar_gates(j + SG_AHEAD, 0)
-            if z_now:
-                apply_gain(j - 2, 1)
-            if sg_now:
-                scalar_gates(j + SG_AHEAD, 1)
-            if o_now:
-                normalise_and_store(j - 3, 0)
+                if not last:
+                    apply_gain(j - 2, 1)
+            if SG_LEAD + j < TILES:
+                scalar_gates(SG_LEAD + j)
             if z_now:
                 sum_squares(j - 2, 0)
-            if flip_now:
-                fetch_a(j + AHEAD)
+            if o_now:
+                normalise(j - 3, 0)
             if z_now:
                 sum_squares(j - 2, 1)
                 inverse_rms(j - 2)
+            if flip_now:
+                fetch_a(j + AHEAD)
             if o_now:
-                normalise_and_store(j - 3, 1)
+                if j - 3 == PAIRS - 1:
+                    normalise_with_gain(j - 3, 1)
+                else:
+                    normalise(j - 3, 1)
             if flip_now:
                 fetch_b(j + AHEAD)

@@ -133,32 +133,36 @@ def tile_selfinteraction_pb_t_kernel(tc, s, v, g_v, wv, ln_g1, out):
 
         def flip_a(j):
             va = va_psum.tile([P, P * PACK], F32, tag="va")
-            bank = va[:].bitcast(BF16)
+            bank = va[:].bitcast(BF16).rearrange("p (d r t b) -> p d t r b", r=P // 2, t=PACK, b=2)
             words = slice(j * P, (j + 1) * P)
             for d in range(DIMS - 1):
                 for t in range(PACK):
-                    b = (d * PACK + t) * P
                     nc.tensor.transpose(
-                        out=bank[:, b : b + P], in_=v_vals[:, words, DIMS * t + d], identity=ident_b[:]
+                        out=bank[:, d, t, :, :], in_=v_vals[:, words, DIMS * t + d], identity=ident_b[:]
                     )
             va_of[j] = va
 
         def flip_b(j):
             vb = flip_psum.tile([P, P * PACK], F32, tag="vb")
-            bank = vb[:].bitcast(BF16)
+            bank = vb[:].bitcast(BF16)[:, 0 : P * PACK].rearrange("p (r t b) -> p t r b", t=PACK, b=2)
             words = slice(j * P, (j + 1) * P)
             for t in range(PACK):
-                nc.tensor.transpose(
-                    out=bank[:, t * P : (t + 1) * P],
-                    in_=v_vals[:, words, DIMS * t + DIMS - 1],
-                    identity=ident_b[:],
+                nc.tensor.matmul(
+                    out=bank[:, t, :, :],
+                    lhsT=v_vals[:, words, DIMS * t + DIMS - 1],
+                    rhs=ident_b[:],
+                    start=True,
+                    stop=True,
                 )
-            for u in range(PACK // 2):
-                b = (2 + u) * P
-                nc.tensor.transpose(out=vb[:, b : b + P], in_=g0_words[:, words, u], identity=ident[:])
             vb_of[j] = vb
 
-        def flip_c(j):
+        def flip_gates(j):
+            words = slice(j * P, (j + 1) * P)
+            for u in range(PACK // 2):
+                b = (2 + u) * P
+                nc.tensor.transpose(
+                    out=vb_of[j][:, b : b + P], in_=g0_words[:, words, u], identity=ident[:]
+                )
             sg_t = flip_psum.tile([P, PACK, P], F32, tag="sg_t")
             for t in range(PACK):
                 nc.tensor.transpose(out=sg_t[:, t, :], in_=sg_of[j][:, t, :], identity=ident[:])
@@ -167,15 +171,15 @@ def tile_selfinteraction_pb_t_kernel(tc, s, v, g_v, wv, ln_g1, out):
         def fetch_a(j):
             v_t = vt_pool.tile([P, DIMS, P, PACK], BF16, tag="v_t")
             nc.scalar.copy(
-                out=v_t[:, 0 : DIMS - 1, :, :],
-                in_=va_of[j][:].bitcast(BF16).rearrange("p (d t n) -> p d n t", t=PACK, n=P),
+                out=v_t[:, 0 : DIMS - 1, :, :].rearrange("p d (r b) t -> p (d r) b t", b=2),
+                in_=va_of[j][:].bitcast(BF16).rearrange("p (q t b) -> p q b t", t=PACK, b=2),
             )
             v_t_of[j] = v_t
 
         def fetch_b(j):
             nc.scalar.copy(
-                out=v_t_of[j][:, DIMS - 1, :, :],
-                in_=vb_of[j][:].bitcast(BF16)[:, 0 : PACK * P].rearrange("p (t n) -> p n t", t=PACK),
+                out=v_t_of[j][:, DIMS - 1, :, :].rearrange("p (r b) t -> p r b t", b=2),
+                in_=vb_of[j][:].bitcast(BF16)[:, 0 : PACK * P].rearrange("p (r t b) -> p r b t", t=PACK, b=2),
             )
 
         def product_0(j):
@@ -302,7 +306,7 @@ def tile_selfinteraction_pb_t_kernel(tc, s, v, g_v, wv, ln_g1, out):
         for j in range(AHEAD):
             flip_a(j)
             flip_b(j)
-            flip_c(j)
+            flip_gates(j)
             fetch_a(j)
             fetch_b(j)
 
@@ -347,7 +351,7 @@ def tile_selfinteraction_pb_t_kernel(tc, s, v, g_v, wv, ln_g1, out):
                 product_1(j)
             if flip_now:
                 flip_b(j + AHEAD)
-                flip_c(j + AHEAD)
+                flip_gates(j + AHEAD)
             if y_now:
                 for d in range(DIMS):
                     residual(j - 1, 0, d)

@@ -28,8 +28,9 @@ PAIRS = TILES // GROUP
 COLUMNS = PARTS * DIMS * P
 EARLY = 2 * P
 AHEAD = 2
-SG_LEAD = 19
-SG_PAIRS = 10
+SG_LEAD = 11
+SG_PAIRS = 6
+LATE_PAIRS = 2
 LOAD_AHEAD = 6
 GATES_AHEAD = 10
 EPS = 1e-6
@@ -158,14 +159,12 @@ def tile_selfinteraction_pb_t_kernel(tc, s, v, g_v, wv, ln_g1, out):
 
         def flip_gates(j):
             words = slice(j * P, (j + 1) * P)
+            g0_t = vb_of[j][:, 2 * P : 4 * P].rearrange("p (n u) -> p n u", u=PACK // 2)
             for u in range(PACK // 2):
-                b = (2 + u) * P
-                nc.tensor.transpose(
-                    out=vb_of[j][:, b : b + P], in_=g0_words[:, words, u], identity=ident[:]
-                )
-            sg_t = flip_psum.tile([P, PACK, P], F32, tag="sg_t")
+                nc.tensor.transpose(out=g0_t[:, :, u], in_=g0_words[:, words, u], identity=ident[:])
+            sg_t = flip_psum.tile([P, P, PACK], F32, tag="sg_t")
             for t in range(PACK):
-                nc.tensor.transpose(out=sg_t[:, t, :], in_=sg_of[j][:, t, :], identity=ident[:])
+                nc.tensor.transpose(out=sg_t[:, :, t], in_=sg_of[j][:, t, :], identity=ident[:])
             sg_t_of[j] = sg_t
 
         def fetch_a(j):
@@ -184,26 +183,29 @@ def tile_selfinteraction_pb_t_kernel(tc, s, v, g_v, wv, ln_g1, out):
 
         def product_0(j):
             u = mx_pool.tile([P, PARTS, DIMS, P * PACK], BF16, align_bytes=64, tag="u")
-            gates = vb_of[j][:].bitcast(BF16)[:, PACK * P : 2 * PACK * P]
-            for d in range(DIMS):
-                nc.vector.tensor_tensor(
-                    out=u[:, 0, d, :].rearrange("p (n u e) -> p n u e", u=2, e=2),
-                    in0=gates.rearrange("p (u n e) -> p n u e", u=2, e=2),
-                    in1=v_t_of[j][:, d, :, :].rearrange("p n (u e) -> p n u e", e=2),
-                    op=MULT,
-                )
+            nc.vector.tensor_tensor(
+                out=u[:, 0, :, :],
+                in0=vb_of[j][:]
+                .bitcast(BF16)[:, PACK * P : 2 * PACK * P]
+                .unsqueeze(1)
+                .to_broadcast([P, DIMS, PACK * P]),
+                in1=v_t_of[j][:].rearrange("p d n t -> p d (n t)"),
+                op=MULT,
+            )
             u_of[j] = u
 
         def product_1(j):
-            for d in range(DIMS):
-                nc.vector.scalar_tensor_tensor(
-                    out=u_of[j][:, 1, d, :].rearrange("p (n t) -> p n t", t=PACK),
-                    in0=sg_t_of[j][:].rearrange("p t n -> p n t"),
-                    scalar=math.sqrt(2.0),
-                    in1=v_t_of[j][:, d, :, :],
-                    op0=MULT,
-                    op1=MULT,
-                )
+            nc.vector.scalar_tensor_tensor(
+                out=u_of[j][:, 1, :, :],
+                in0=sg_t_of[j][:]
+                .rearrange("p n t -> p (n t)")
+                .unsqueeze(1)
+                .to_broadcast([P, DIMS, P * PACK]),
+                scalar=math.sqrt(2.0),
+                in1=v_t_of[j][:].rearrange("p d n t -> p d (n t)"),
+                op0=MULT,
+                op1=MULT,
+            )
 
         def quantise(j, first, last):
             if first == 0:
@@ -267,13 +269,16 @@ def tile_selfinteraction_pb_t_kernel(tc, s, v, g_v, wv, ln_g1, out):
             inv_rms_of[j] = inv_rms
 
         def apply_gain(j, k):
-            o = o_pool.tile([P, DIMS, C], F32, tag="o")
-            nc.gpsimd.tensor_tensor(
-                out=o[:],
-                in0=y_of[j][:, k, :, :],
-                in1=gain_sb[:].unsqueeze(1).to_broadcast([P, DIMS, C]),
-                op=MULT,
-            )
+            o = o_pool.tile([P, C * DIMS], F32, tag="o")
+            y = y_of[j][:, k, :, :]
+            if k == 0:
+                o_view = o[:].rearrange("p (d c) -> p d c", d=DIMS)
+                gain = gain_sb[:].unsqueeze(1).to_broadcast([P, DIMS, C])
+            else:
+                o_view = o[:].rearrange("p (c d) -> p c d", d=DIMS)
+                y = y.rearrange("p d c -> p c d")
+                gain = gain_sb[:].unsqueeze(2).to_broadcast([P, C, DIMS])
+            nc.gpsimd.tensor_tensor(out=o_view, in0=y, in1=gain, op=MULT)
             o_of[(j, k)] = o
 
         def store(j, k, z):
@@ -281,12 +286,11 @@ def tile_selfinteraction_pb_t_kernel(tc, s, v, g_v, wv, ln_g1, out):
 
         def normalise(j, k):
             z = z_pool.tile([P, C, DIMS], F32, tag="z")
-            nc.scalar.activation(
-                out=z[:],
-                in_=o_of[(j, k)][:].rearrange("p d c -> p c d"),
-                func=ACT.Copy,
-                scale=inv_rms_of[j][:, k : k + 1],
-            )
+            if k == 0:
+                o_view = o_of[(j, k)][:].rearrange("p (d c) -> p c d", d=DIMS)
+            else:
+                o_view = o_of[(j, k)][:].rearrange("p (c d) -> p c d", d=DIMS)
+            nc.scalar.activation(out=z[:], in_=o_view, func=ACT.Copy, scale=inv_rms_of[j][:, k : k + 1])
             store(j, k, z)
 
         def normalise_with_gain(j, k):
@@ -326,6 +330,7 @@ def tile_selfinteraction_pb_t_kernel(tc, s, v, g_v, wv, ln_g1, out):
             in_=w_grouped[:].rearrange("q o c t -> q (o c t)"),
         )
 
+        sg_made = SG_LEAD
         for j in range(PAIRS + 3):
             now = j < PAIRS
             y_now = 0 <= j - 1 < PAIRS
@@ -357,26 +362,24 @@ def tile_selfinteraction_pb_t_kernel(tc, s, v, g_v, wv, ln_g1, out):
                     residual(j - 1, 0, d)
             if now:
                 quantise(j, EARLY, COLUMNS)
-            last = j - 2 == PAIRS - 1
-            if z_now:
-                apply_gain(j - 2, 0)
-                if not last:
-                    apply_gain(j - 2, 1)
-            if SG_LEAD + j < TILES:
-                scalar_gates(SG_LEAD + j)
+            if z_now and j - 2 < PAIRS - LATE_PAIRS:
+                for k in range(GROUP):
+                    apply_gain(j - 2, k)
+            for i in range(2 if j < PAIRS // 2 else 1):
+                if sg_made < TILES:
+                    scalar_gates(sg_made)
+                    sg_made += 1
+            finish = normalise if j - 3 < PAIRS - LATE_PAIRS else normalise_with_gain
+            if o_now:
+                finish(j - 3, 0)
             if z_now:
                 sum_squares(j - 2, 0)
-            if o_now:
-                normalise(j - 3, 0)
+            if flip_now:
+                fetch_a(j + AHEAD)
             if z_now:
                 sum_squares(j - 2, 1)
                 inverse_rms(j - 2)
-            if flip_now:
-                fetch_a(j + AHEAD)
             if o_now:
-                if j - 3 == PAIRS - 1:
-                    normalise_with_gain(j - 3, 1)
-                else:
-                    normalise(j - 3, 1)
+                finish(j - 3, 1)
             if flip_now:
                 fetch_b(j + AHEAD)

import math
from contextlib import ExitStack

import concourse.mybir as mybir
from concourse.masks import make_identity

BF16 = mybir.dt.bfloat16
F32 = mybir.dt.float32
U32 = mybir.dt.uint32
U8 = mybir.dt.uint8
FP8X4 = mybir.dt.float8_e4m3fn_x4
MULT = mybir.AluOpType.mult
ADD = mybir.AluOpType.add
ACT = mybir.ActivationFunctionType

P = 128
HALF = P // 2
POINTS = 4096
C = 256
DIMS = 3
KV = 2 * C
PACK = 4
WORDS = C // PACK
PARTS = 2
TILES = POINTS // P
GROUP = 2
PAIRS = TILES // GROUP
COLUMNS = PARTS * DIMS * P
EARLY = 2 * P
AHEAD = 2
SG_LEAD = 11
SG_PAIRS = 6
LATE_PAIRS = 2
LOAD_AHEAD = 6
GATES_AHEAD = 10
EPS = 1e-6

FLOPS = 2 * POINTS * DIMS * KV * C


def tile_selfinteraction_pb_t_kernel(tc, s, v, g_v, wv, ln_g1, out):
    nc = tc.nc
    with ExitStack() as ctx:
        const = ctx.enter_context(tc.tile_pool(name="const", bufs=1))
        sg_pool = ctx.enter_context(tc.tile_pool(name="sg_pool", bufs=SG_PAIRS))
        vt_pool = ctx.enter_context(tc.tile_pool(name="vt_pool", bufs=3))
        mx_pool = ctx.enter_context(tc.tile_pool(name="mx_pool", bufs=2))
        y_pool = ctx.enter_context(tc.tile_pool(name="y_pool", bufs=4))
        o_pool = ctx.enter_context(tc.tile_pool(name="o_pool", bufs=5))
        z_pool = ctx.enter_context(tc.tile_pool(name="z_pool", bufs=5))
        stat_pool = ctx.enter_context(tc.tile_pool(name="stat_pool", bufs=3))
        va_psum = ctx.enter_context(tc.psum_pool(name="va_psum", bufs=1))
        flip_psum = ctx.enter_context(tc.psum_pool(name="flip_psum", bufs=2))
        dv_psum = ctx.enter_context(tc.psum_pool(name="dv_psum", bufs=DIMS))
        ctx.enter_context(tc.manual_schedule())

        s_dram = s.rearrange("(p i) c -> p i c", i=TILES)
        g_dram = g_v.rearrange("(p i) m -> p i m", i=TILES)
        v_dram = v.rearrange("(p i) c d -> p i (c d)", i=TILES)
        out_dram = out.rearrange("(p i) c d -> p i c d", i=TILES)

        s_sb = const.tile([P, TILES, C], BF16)
        g0_sb = const.tile([P, TILES, C], BF16)
        g1_sb = const.tile([P, TILES, C], BF16)
        v_sb = const.tile([P, TILES, C * DIMS], BF16)
        gain_sb = const.tile([P, C], BF16)
        w_rows = const.tile([P, PACK, C], BF16)
        w_rows_swapped = const.tile([P, PACK, C], BF16)

        def load_gates(first, last):
            tiles = slice(first * GROUP, last * GROUP)
            nc.sync.dma_start(out=s_sb[:, tiles, :], in_=s_dram[:, tiles, :])
            nc.sync.dma_start(out=g1_sb[:, tiles, :], in_=g_dram[:, tiles, C:KV])

        def load_vectors(j):
            tiles = slice(j * GROUP, (j + 1) * GROUP)
            nc.sync.dma_start(out=v_sb[:, tiles, :], in_=v_dram[:, tiles, :])
            nc.sync.dma_start(out=g0_sb[:, tiles, :], in_=g_dram[:, tiles, 0:C])

        load_gates(0, 1)
        load_vectors(0)
        wv_view = wv.rearrange("(p t) c -> p t c", t=PACK)
        nc.sync.dma_start(out=w_rows[:], in_=wv_view)
        nc.sync.dma_start(out=w_rows_swapped[0:HALF], in_=wv_view[HALF:P])
        nc.sync.dma_start(out=w_rows_swapped[HALF:P], in_=wv_view[0:HALF])
        load_gates(1, 2)
        load_vectors(1)
        for j in range(2, LOAD_AHEAD):
            load_gates(2 * j - 2, 2 * j)
            load_vectors(j)
            if j == 3:
                nc.sync.dma_start(out=gain_sb[:], in_=ln_g1.partition_broadcast(P))

        v_vals = v_sb[:].rearrange("p i (q f) -> p (i q) f", f=PACK * DIMS)
        v_cd = v_sb[:].rearrange("p i (c d) -> p i c d", d=DIMS)
        g0_words = g0_sb[:].bitcast(F32).rearrange("p i (q u) -> p (i q) u", u=PACK // 2)

        ident_b = const.tile([P, P], BF16)
        make_identity(nc, ident_b[:])
        ident = const.tile([P, P], F32)
        make_identity(nc, ident[:])
        eps_sb = const.tile([P, 1], F32)
        nc.vector.memset(eps_sb[:], EPS)
        w_grouped = const.tile([P, PARTS * GROUP, C, PACK], BF16, align_bytes=64)
        nc.vector.memset(w_grouped[:], 0.0)
        table_warmer = const.tile([P, 1], F32)
        nc.scalar.activation(out=table_warmer[:], in_=eps_sb[:], func=ACT.Abs_reciprocal_sqrt)

        sg_of = {}
        va_of = {}
        vb_of = {}
        sg_t_of = {}
        v_t_of = {}
        u_of = {}
        u_codes_of = {}
        u_scales_of = {}
        dv_of = {}
        y_of = {}
        o_of = {}
        sum_sq_of = {}
        inv_rms_of = {}

        def scalar_gates(i):
            j, k = divmod(i, GROUP)
            if k == 0:
                sg = sg_pool.tile([P, PACK, P], F32, tag="sg")
                sg_of[j] = sg
            nc.gpsimd.tensor_tensor(
                out=sg_of[j][:, :, k * WORDS : (k + 1) * WORDS],
                in0=s_sb[:, i, :].rearrange("p (q t) -> p t q", t=PACK),
                in1=g1_sb[:, i, :].rearrange("p (q t) -> p t q", t=PACK),
                op=MULT,
            )

        def flip_a(j):
            va = va_psum.tile([P, P * PACK], F32, tag="va")
            bank = va[:].bitcast(BF16).rearrange("p (d r t b) -> p d t r b", r=P // 2, t=PACK, b=2)
            words = slice(j * P, (j + 1) * P)
            for d in range(DIMS - 1):
                for t in range(PACK):
                    nc.tensor.transpose(
                        out=bank[:, d, t, :, :], in_=v_vals[:, words, DIMS * t + d], identity=ident_b[:]
                    )
            va_of[j] = va

        def flip_b(j):
            vb = flip_psum.tile([P, P * PACK], F32, tag="vb")
            bank = vb[:].bitcast(BF16)[:, 0 : P * PACK].rearrange("p (r t b) -> p t r b", t=PACK, b=2)
            words = slice(j * P, (j + 1) * P)
            for t in range(PACK):
                nc.tensor.matmul(
                    out=bank[:, t, :, :],
                    lhsT=v_vals[:, words, DIMS * t + DIMS - 1],
                    rhs=ident_b[:],
                    start=True,
                    stop=True,
                )
            vb_of[j] = vb

        def flip_gates(j):
            words = slice(j * P, (j + 1) * P)
            g0_t = vb_of[j][:, 2 * P : 4 * P].rearrange("p (n u) -> p n u", u=PACK // 2)
            for u in range(PACK // 2):
                nc.tensor.transpose(out=g0_t[:, :, u], in_=g0_words[:, words, u], identity=ident[:])
            sg_t = flip_psum.tile([P, P, PACK], F32, tag="sg_t")
            for t in range(PACK):
                nc.tensor.transpose(out=sg_t[:, :, t], in_=sg_of[j][:, t, :], identity=ident[:])
            sg_t_of[j] = sg_t

        def fetch_a(j):
            v_t = vt_pool.tile([P, DIMS, P, PACK], BF16, tag="v_t")
            nc.scalar.copy(
                out=v_t[:, 0 : DIMS - 1, :, :].rearrange("p d (r b) t -> p (d r) b t", b=2),
                in_=va_of[j][:].bitcast(BF16).rearrange("p (q t b) -> p q b t", t=PACK, b=2),
            )
            v_t_of[j] = v_t

        def fetch_b(j):
            nc.scalar.copy(
                out=v_t_of[j][:, DIMS - 1, :, :].rearrange("p (r b) t -> p r b t", b=2),
                in_=vb_of[j][:].bitcast(BF16)[:, 0 : PACK * P].rearrange("p (r t b) -> p r b t", t=PACK, b=2),
            )

        def product_0(j):
            u = mx_pool.tile([P, PARTS, DIMS, P * PACK], BF16, align_bytes=64, tag="u")
            nc.vector.tensor_tensor(
                out=u[:, 0, :, :],
                in0=vb_of[j][:]
                .bitcast(BF16)[:, PACK * P : 2 * PACK * P]
                .unsqueeze(1)
                .to_broadcast([P, DIMS, PACK * P]),
                in1=v_t_of[j][:].rearrange("p d n t -> p d (n t)"),
                op=MULT,
            )
            u_of[j] = u

        def product_1(j):
            nc.vector.scalar_tensor_tensor(
                out=u_of[j][:, 1, :, :],
                in0=sg_t_of[j][:]
                .rearrange("p n t -> p (n t)")
                .unsqueeze(1)
                .to_broadcast([P, DIMS, P * PACK]),
                scalar=math.sqrt(2.0),
                in1=v_t_of[j][:].rearrange("p d n t -> p d (n t)"),
                op0=MULT,
                op1=MULT,
            )

        def quantise(j, first, last):
            if first == 0:
                codes = mx_pool.tile([P, COLUMNS], U32, align_bytes=64, tag="codes")
                scales = mx_pool.tile([P, COLUMNS], U8, align_bytes=64, tag="scales")
                u_codes_of[j] = codes
                u_scales_of[j] = scales
            nc.vector.quantize_mx(
                out=u_codes_of[j][:, first:last].bitcast(FP8X4),
                scales=u_scales_of[j][:, first:last],
                in_=u_of[j][:].rearrange("p h d w -> p (h d w)")[:, first * PACK : last * PACK],
            )

        def project(j, d):
            dv = dv_psum.tile([P, GROUP, C], F32, tag="dv")
            for h in range(PARTS):
                cols = slice((h * DIMS + d) * P, (h * DIMS + d + 1) * P)
                w_cols = slice(h * GROUP * C, (h + 1) * GROUP * C)
                nc.tensor.matmul_mx(
                    out=dv[:].rearrange("p k c -> p (k c)"),
                    lhsT=u_codes_of[j][:, cols].bitcast(FP8X4),
                    lhsT_scale=u_scales_of[j][:, cols],
                    rhs=wv_codes[:, w_cols].bitcast(FP8X4),
                    rhs_scale=wv_scales[:, w_cols],
                    start=(h == 0),
                    stop=(h == PARTS - 1),
                )
            dv_of[(j, d)] = dv

        def residual(j, k, d):
            if k == 0 and d == 0:
                y = y_pool.tile([P, GROUP, DIMS, C], F32, tag="y")
                y_of[j] = y
            nc.vector.scalar_tensor_tensor(
                out=y_of[j][:, k, d, :],
                in0=dv_of[(j, d)][:, k, :],
                scalar=1.0 / math.sqrt(KV),
                in1=v_cd[:, j * GROUP + k, :, d],
                op0=MULT,
                op1=ADD,
            )

        def sum_squares(j, k):
            if k == 0:
                sum_sq = stat_pool.tile([P, GROUP], F32, tag="sum_sq")
                sum_sq_of[j] = sum_sq
            squares = stat_pool.tile([P, DIMS, C], BF16, tag="squares")
            nc.scalar.activation(
                out=squares[:], in_=y_of[j][:, k, :, :], func=ACT.Square, accum_out=sum_sq_of[j][:, k : k + 1]
            )

        def inverse_rms(j):
            inv_rms = stat_pool.tile([P, GROUP], F32, tag="inv_rms")
            nc.scalar.activation(
                out=inv_rms[:],
                in_=sum_sq_of[j][:],
                func=ACT.Abs_reciprocal_sqrt,
                bias=eps_sb[:],
                scale=1.0 / (C * DIMS),
            )
            inv_rms_of[j] = inv_rms

        def apply_gain(j, k):
            o = o_pool.tile([P, C * DIMS], F32, tag="o")
            y = y_of[j][:, k, :, :]
            if k == 0:
                o_view = o[:].rearrange("p (d c) -> p d c", d=DIMS)
                gain = gain_sb[:].unsqueeze(1).to_broadcast([P, DIMS, C])
            else:
                o_view = o[:].rearrange("p (c d) -> p c d", d=DIMS)
                y = y.rearrange("p d c -> p c d")
                gain = gain_sb[:].unsqueeze(2).to_broadcast([P, C, DIMS])
            nc.gpsimd.tensor_tensor(out=o_view, in0=y, in1=gain, op=MULT)
            o_of[(j, k)] = o

        def store(j, k, z):
            nc.sync.dma_start(out=out_dram[:, j * GROUP + k, :, :], in_=z[:])

        def normalise(j, k):
            z = z_pool.tile([P, C, DIMS], F32, tag="z")
            if k == 0:
                o_view = o_of[(j, k)][:].rearrange("p (d c) -> p c d", d=DIMS)
            else:
                o_view = o_of[(j, k)][:].rearrange("p (c d) -> p c d", d=DIMS)
            nc.scalar.activation(out=z[:], in_=o_view, func=ACT.Copy, scale=inv_rms_of[j][:, k : k + 1])
            store(j, k, z)

        def normalise_with_gain(j, k):
            z = z_pool.tile([P, C, DIMS], F32, tag="z")
            nc.vector.scalar_tensor_tensor(
                out=z[:],
                in0=y_of[j][:, k, :, :].rearrange("p d c -> p c d"),
                scalar=inv_rms_of[j][:, k : k + 1],
                in1=gain_sb[:].unsqueeze(2).to_broadcast([P, C, DIMS]),
                op0=MULT,
                op1=MULT,
            )
            store(j, k, z)

        for i in range(SG_LEAD):
            scalar_gates(i)
        for j in range(AHEAD):
            flip_a(j)
            flip_b(j)
            flip_gates(j)
            fetch_a(j)
            fetch_b(j)

        for h in range(PARTS):
            for k in range(GROUP):
                rows = slice(k * HALF, (k + 1) * HALF)
                source = w_rows if h == k else w_rows_swapped
                nc.vector.tensor_copy(
                    out=w_grouped[rows, h * GROUP + k, :, :],
                    in_=source[rows, :, :].rearrange("q t c -> q c t"),
                )
        wv_codes = const.tile([P, PARTS * GROUP * C], U32, align_bytes=64)
        wv_scales = const.tile([P, PARTS * GROUP * C], U8, align_bytes=64)
        nc.vector.quantize_mx(
            out=wv_codes[:].bitcast(FP8X4),
            scales=wv_scales[:],
            in_=w_grouped[:].rearrange("q o c t -> q (o c t)"),
        )

        sg_made = SG_LEAD
        for j in range(PAIRS + 3):
            now = j < PAIRS
            y_now = 0 <= j - 1 < PAIRS
            z_now = 0 <= j - 2 < PAIRS
            o_now = 0 <= j - 3 < PAIRS
            flip_now = j + AHEAD < PAIRS
            if j + LOAD_AHEAD < PAIRS:
                load_vectors(j + LOAD_AHEAD)
            if j + GATES_AHEAD < PAIRS:
                load_gates(j + GATES_AHEAD, j + GATES_AHEAD + 1)
            if flip_now:
                flip_a(j + AHEAD)
            if now:
                product_0(j)
            if z_now:
                for d in range(DIMS):
                    residual(j - 2, 1, d)
            if y_now:
                for d in range(DIMS):
                    project(j - 1, d)
            if now:
                quantise(j, 0, EARLY)
                product_1(j)
            if flip_now:
                flip_b(j + AHEAD)
                flip_gates(j + AHEAD)
            if y_now:
                for d in range(DIMS):
                    residual(j - 1, 0, d)
            if now:
                quantise(j, EARLY, COLUMNS)
            if z_now and j - 2 < PAIRS - LATE_PAIRS:
                for k in range(GROUP):
                    apply_gain(j - 2, k)
            for i in range(2 if j < PAIRS // 2 else 1):
                if sg_made < TILES:
                    scalar_gates(sg_made)
                    sg_made += 1
            finish = normalise if j - 3 < PAIRS - LATE_PAIRS else normalise_with_gain
            if o_now:
                finish(j - 3, 0)
            if z_now:
                sum_squares(j - 2, 0)
            if flip_now:
                fetch_a(j + AHEAD)
            if z_now:
                sum_squares(j - 2, 1)
                inverse_rms(j - 2)
            if o_now:
                finish(j - 3, 1)
            if flip_now:
                fetch_b(j + AHEAD)
